import numpy as np
import ml_dtypes


def mxq(x, axis, fmt="e4m3"):
    dtype, down = {"e4m3": (ml_dtypes.float8_e4m3fn, 7), "e5m2": (ml_dtypes.float8_e5m2, 14)}[fmt]
    v = np.moveaxis(np.asarray(x, np.float32).astype(ml_dtypes.bfloat16).astype(np.float64), axis, -1)
    blocks = v.reshape(v.shape[:-1] + (-1, 32))
    amax = np.abs(blocks).max(-1, keepdims=True)
    byte = np.maximum(np.where(amax > 0, np.frexp(amax)[1] - 1 + 127, 0) - down, 1)
    scale = np.exp2(byte - 127.0)
    codes = (blocks / scale).astype(np.float32).astype(dtype).astype(np.float64)
    return np.moveaxis((codes * scale).reshape(v.shape), -1, axis)


WIDE = False


def mx_kscale(k):
    if not WIDE:
        return np.ones(k)
    levels = np.array([10, -10, 5, -5, 0])
    a = np.random.permutation(np.resize(levels, k // 512 * 4)).reshape(k // 512, 4)
    idx = np.arange(k)
    return np.exp2(a[idx // 512, idx % 128 // 32])


BF16 = ml_dtypes.bfloat16


def bf(x):
    return np.asarray(x, np.float32).astype(BF16)


def f64(x):
    return np.asarray(x).astype(np.float64)


E2M1 = np.array([0.0, 0.5, 1.0, 1.5, 2.0, 3.0, 4.0, 6.0, -0.0, -0.5, -1.0, -1.5, -2.0, -3.0, -4.0, -6.0])


def pack_weight(w, fmt):
    k, n = w.shape
    w = f64(bf(w)).reshape(k // 32, 32, n)
    amax = np.abs(w).max(1)
    if fmt == "e4m3":
        byte = np.frexp(amax)[1] - 1 + 127 - 7
    else:
        mant, ex = np.frexp(amax / 6.0)
        byte = np.where(mant > 0.5, ex, ex - 1) + 127
    byte = np.clip(np.where(amax > 0, byte, 1), 1, 254)
    scaled = (w * np.exp2(127.0 - byte)[:, None, :]).reshape(k, n).astype(np.float32)
    by_word = np.ascontiguousarray(scaled.reshape(k // 512, 128, 4, n).transpose(0, 1, 3, 2))
    if fmt == "e4m3":
        words = by_word.astype(ml_dtypes.float8_e4m3fn).view(np.uint8)
    else:
        c = by_word.astype(ml_dtypes.float4_e2m1fn).view(np.uint8) & 0xF
        words = c[..., 0::2] | (c[..., 1::2] << 4)
    return np.ascontiguousarray(words), np.ascontiguousarray(byte.astype(np.uint8).reshape(k // 512, 16, n))


def unpack_weight(words, scales, fmt):
    g, p, n, _ = words.shape
    if fmt == "e4m3":
        vals = np.ascontiguousarray(words).view(ml_dtypes.float8_e4m3fn).astype(np.float64)
    else:
        nib = np.empty((g, p, n, 4), np.uint8)
        nib[..., 0::2] = words & 0xF
        nib[..., 1::2] = words >> 4
        vals = E2M1[nib]
    vals = vals * np.repeat(np.exp2(scales.astype(np.float64) - 127.0), 8, axis=1)[..., None]
    return vals.transpose(0, 1, 3, 2).reshape(g * 512, n)


N, D, H = 1024, 2048, 1024
LN_EPS = 1e-5
ERF_TERMS = 120
FMT = "e4m3"


def erf(x):
    a = np.clip(x, -6.0, 6.0)
    term = a
    total = a
    for n in range(1, ERF_TERMS):
        term = term * (2.0 * a * a / (2.0 * n + 1.0))
        total = total + term
    return 2.0 / np.sqrt(np.pi) * np.exp(-a * a) * total


def gelu(v):
    return 0.5 * v * (1.0 + erf(v / np.sqrt(2.0)))


def layernorm(x, g, b):
    m = x.mean(-1, keepdims=True)
    v = np.square(x - m).mean(-1, keepdims=True)
    return (x - m) / np.sqrt(v + LN_EPS) * g + b


def setup_inputs():
    s = mx_kscale(H)
    h1 = bf(gelu(np.random.standard_normal((N, H))) * s)
    w2_deq = np.random.standard_normal((H, H)) * 1.5 / np.sqrt(H) / s
    w2_deq_words, w2_deq_scales = pack_weight(np.ascontiguousarray(w2_deq.T), FMT)
    b2 = bf(0.1 * np.random.standard_normal(H))
    g2 = bf(1.0 + 0.1 * np.random.standard_normal(H))
    b2_ln = bf(0.1 * np.random.standard_normal(H))
    Wo = np.random.standard_normal((D, H)) * 1.5 / np.sqrt(H)
    Wo_words, Wo_scales = pack_weight(np.ascontiguousarray(Wo.T), FMT)
    bo = bf(0.1 * np.random.standard_normal(D))
    return {
        "h1": h1,
        "w2_deq_words": w2_deq_words,
        "w2_deq_scales": w2_deq_scales,
        "b2": b2,
        "g2": g2,
        "b2_ln": b2_ln,
        "Wo_words": Wo_words,
        "Wo_scales": Wo_scales,
        "bo": bo,
    }


def reference(h1, w2_deq_words, w2_deq_scales, b2, g2, b2_ln, Wo_words, Wo_scales, bo):
    y = (mxq(f64(h1), 1, "e4m3") @ unpack_weight(w2_deq_words, w2_deq_scales, FMT)) + f64(b2)
    h2 = gelu(layernorm(y, f64(g2), f64(b2_ln)))
    return (mxq(h2, 1, "e4m3") @ unpack_weight(Wo_words, Wo_scales, FMT)) + f64(bo)

@@ -1,0 +1,278 @@
+from contextlib import ExitStack
+
+import concourse.mybir as mybir
+from concourse.masks import make_identity
+
+F32 = mybir.dt.float32
+BF16 = mybir.dt.bfloat16
+I32 = mybir.dt.int32
+U32 = mybir.dt.uint32
+U8 = mybir.dt.uint8
+FP8X4 = mybir.dt.float8_e4m3fn_x4
+ACT = mybir.ActivationFunctionType
+ALU = mybir.AluOpType
+
+P = 128
+PACK = 4
+K_PASS = P * PACK
+N_TILE = 512
+TOKENS = 1024
+HIDDEN = 1024
+OUT_DIM = 2048
+LN_EPS = 1e-5
+PASSES = HIDDEN // K_PASS
+TOKEN_TILES = TOKENS // P
+PAIR = 2
+PAIR_TOKENS = PAIR * P
+UNITS = (TOKEN_TILES // PAIR) * PASSES
+GELU_LAG = 4
+QUANT_LAG = GELU_LAG + 1
+OUT_LAG = QUANT_LAG + 1
+
+FLOPS = 2 * TOKENS * HIDDEN * HIDDEN + 2 * TOKENS * HIDDEN * OUT_DIM
+
+
+def tile_synapsemodel_pb_kernel(
+    tc, h1, w2_deq_words, w2_deq_scales, b2, g2, b2_ln, Wo_words, Wo_scales, bo, out
+):
+    nc = tc.nc
+    with ExitStack() as ctx:
+        const = ctx.enter_context(tc.tile_pool(name="const", bufs=1))
+        keep = ctx.enter_context(tc.tile_pool(name="keep", bufs=1))
+        stage = ctx.enter_context(tc.tile_pool(name="stage", bufs=3))
+        rows = ctx.enter_context(tc.tile_pool(name="rows", bufs=4))
+        stats = ctx.enter_context(tc.tile_pool(name="stats", bufs=4))
+        results = ctx.enter_context(tc.tile_pool(name="results", bufs=3))
+        transposed = ctx.enter_context(tc.psum_pool(name="transposed", bufs=4))
+        products = ctx.enter_context(tc.psum_pool(name="products", bufs=4))
+        ctx.enter_context(tc.manual_schedule())
+
+        w2_words = const.tile([P, PASSES, HIDDEN], U32, align_bytes=64)
+        w2_planes = const.tile([P, PASSES, HIDDEN], U8, align_bytes=64)
+        wo_words = const.tile([P, PASSES, OUT_DIM], U32, align_bytes=64)
+        wo_planes = const.tile([P, PASSES, OUT_DIM], U8, align_bytes=64)
+        nc.vector.memset(w2_planes[:].bitcast(I32), 0)
+        nc.vector.memset(wo_planes[:].bitcast(I32), 0)
+
+        def load_words(words, dram, cols):
+            source = dram.rearrange("g p n t -> p g (n t)").bitcast(I32)
+            nc.sync.dma_start(out=words[:, :, cols].bitcast(I32), in_=source[:, :, cols])
+
+        def load_scale_rows(planes, dram):
+            source = dram.bitcast(I32)
+            for quadrant in range(4):
+                nc.sync.dma_start(
+                    out=planes[32 * quadrant : 32 * quadrant + 4].bitcast(I32),
+                    in_=source[:, 4 * quadrant : 4 * quadrant + 4, :].rearrange("g r n -> r g n"),
+                )
+
+        h1_tiles = h1.rearrange("(i r) k -> i r k", r=P)
+        h1_sb = []
+        for i in range(TOKEN_TILES):
+            h1_tile = const.tile([P, HIDDEN], BF16, name="h1_tile_%d" % i)
+            h1_sb.append(h1_tile)
+
+        def load_h1(i):
+            nc.sync.dma_start(out=h1_sb[i][:], in_=h1_tiles[i])
+
+        load_h1(0)
+        load_h1(1)
+        load_words(w2_words, w2_deq_words, slice(0, N_TILE))
+        load_scale_rows(w2_planes, w2_deq_scales)
+        load_words(w2_words, w2_deq_words, slice(N_TILE, HIDDEN))
+        for i in range(2, TOKEN_TILES):
+            load_h1(i)
+        load_scale_rows(wo_planes, Wo_scales)
+        load_words(wo_words, Wo_words, slice(0, OUT_DIM // 2))
+        load_words(wo_words, Wo_words, slice(OUT_DIM // 2, OUT_DIM))
+        bo_rows = const.tile([P, OUT_DIM], BF16)
+        nc.sync.dma_start(out=bo_rows[:], in_=bo.partition_broadcast(P))
+
+        identity = const.tile([P, P], F32)
+        make_identity(nc, identity[:])
+        minus_half = const.tile([P, 1], F32)
+        nc.gpsimd.memset(minus_half[:], -0.5)
+
+        b2_rows = const.tile([P, HIDDEN], BF16)
+        nc.scalar.dma_start(out=b2_rows[:], in_=b2.partition_broadcast(P))
+        b2_sorted = const.tile([P, PASSES, PACK, P], F32)
+        nc.vector.tensor_copy(
+            out=b2_sorted[:], in_=b2_rows[:].rearrange("r (g q t) -> r g t q", g=PASSES, t=PACK)
+        )
+
+        def load_per_k(vector, name):
+            as_bf16 = const.tile([P, PASSES, PACK], BF16, name=name + "_bf16")
+            with nc.allow_non_contiguous_dma(reason="8-byte runs of a 2 KiB vector, once"):
+                nc.scalar.dma_start(
+                    out=as_bf16[:], in_=vector.rearrange("(g q t) -> q g t", g=PASSES, t=PACK)
+                )
+            as_f32 = const.tile([P, PASSES, PACK], F32, name=name)
+            nc.gpsimd.tensor_copy(out=as_f32[:], in_=as_bf16[:])
+            return as_f32
+
+        gain = load_per_k(g2, "gain")
+        shift = load_per_k(b2_ln, "shift")
+
+        h1_codes = keep.tile([P, TOKEN_TILES, PASSES * P], U32, align_bytes=64)
+        h1_scales = keep.tile([P, TOKEN_TILES, PASSES * P], U8, align_bytes=64)
+        h2_codes = keep.tile([P, PASSES, TOKENS], U32, align_bytes=64)
+        h2_scales = keep.tile([P, PASSES, TOKENS], U8, align_bytes=64)
+        normalised = {}
+
+        def flip_h1(i):
+            pairs_of_k = h1_sb[i][:].bitcast(F32)
+            flipped = transposed.tile([P, PASSES, 2, P], F32, tag="bank")
+            for g in range(PASSES):
+                for u in range(2):
+                    nc.tensor.transpose(
+                        flipped[:, g, u, :],
+                        pairs_of_k[:, 256 * g + u : 256 * (g + 1) : 2],
+                        identity[:],
+                    )
+            grouped = stage.tile([P, PASSES, P, PACK], BF16, align_bytes=64)
+            nc.scalar.copy(
+                out=grouped[:].bitcast(F32), in_=flipped[:].rearrange("q g u r -> q g r u")
+            )
+            return grouped
+
+        def quantise_h1(i, grouped):
+            nc.vector.quantize_mx(
+                out=h1_codes[:, i, :].bitcast(FP8X4),
+                scales=h1_scales[:, i, :],
+                in_=grouped[:].rearrange("q g r t -> q (g r t)"),
+            )
+
+        def first_matmul(i):
+            y = rows.tile([P, PASSES, PACK, P], F32)
+            row_sum = stats.tile([P, PASSES], F32)
+            for chunk in range(HIDDEN // N_TILE):
+                cols = slice(chunk * N_TILE, (chunk + 1) * N_TILE)
+                acc = products.tile([P, N_TILE], F32, tag="bank")
+                for g in range(PASSES):
+                    of_pass = slice(g * P, (g + 1) * P)
+                    nc.tensor.matmul_mx(
+                        out=acc[:],
+                        lhsT=h1_codes[:, i, of_pass].bitcast(FP8X4),
+                        lhsT_scale=h1_scales[:, i, of_pass],
+                        rhs=w2_words[:, g, cols].bitcast(FP8X4),
+                        rhs_scale=w2_planes[:, g, cols],
+                        start=(g == 0),
+                        stop=(g == PASSES - 1),
+                    )
+                nc.vector.scalar_tensor_tensor(
+                    out=y[:, chunk],
+                    in0=acc[:].rearrange("r (q t) -> r t q", t=PACK),
+                    scalar=1.0,
+                    in1=b2_sorted[:, chunk],
+                    op0=ALU.mult,
+                    op1=ALU.add,
+                    accum_out=row_sum[:, chunk : chunk + 1],
+                )
+            return y, row_sum
+
+        def normalise(i, y, row_sum):
+            flat = y[:].rearrange("r g t q -> r (g t q)")
+            neg_mean = stats.tile([P, 1], F32)
+            nc.vector.tensor_scalar(
+                out=neg_mean[:],
+                in0=row_sum[:, 0:1],
+                scalar1=row_sum[:, 1:2],
+                scalar2=-1.0 / HIDDEN,
+                op0=ALU.add,
+                op1=ALU.mult,
+            )
+            squares = rows.tile([P, HIDDEN], BF16)
+            sum_sq = stats.tile([P, 1], F32)
+            nc.scalar.activation(
+                out=squares[:], in_=flat, func=ACT.Square, bias=neg_mean[:], scale=1.0,
+                accum_out=sum_sq[:],
+            )
+            var_eps = stats.tile([P, 1], F32)
+            nc.gpsimd.tensor_scalar(
+                out=var_eps[:], in0=sum_sq[:], scalar1=1.0 / HIDDEN, scalar2=LN_EPS,
+                op0=ALU.mult, op1=ALU.add,
+            )
+            rstd = stats.tile([P, 1], F32)
+            nc.gpsimd.tensor_tensor(out=rstd[:], in0=var_eps[:], in1=minus_half[:], op=ALU.pow)
+            centred = rows.tile([P, PASSES, PACK, P], F32, bufs=6)
+            nc.gpsimd.tensor_scalar(
+                out=centred[:].rearrange("r g t q -> r (g t q)"), in0=flat,
+                scalar1=neg_mean[:], scalar2=rstd[:], op0=ALU.add, op1=ALU.mult,
+            )
+            normalised[i] = centred
+
+        def gelu_unit(unit):
+            j, g = divmod(unit, PASSES)
+            h2_by_t = stage.tile([P, PACK, PAIR_TOKENS], BF16)
+            banks = []
+            for half in range(2):
+                flipped = transposed.tile([P, 2, PAIR_TOKENS], F32, tag="bank")
+                banks.append(flipped)
+                for u in range(2):
+                    for s in range(PAIR):
+                        nc.tensor.transpose(
+                            flipped[:, u, s * P : (s + 1) * P],
+                            normalised[PAIR * j + s][:, g, 2 * half + u, :],
+                            identity[:],
+                        )
+            for t in range(PACK):
+                nc.scalar.activation(
+                    out=h2_by_t[:, t, :], in_=banks[t // 2][:, t % 2, :], func=ACT.Gelu,
+                    bias=shift[:, g, t : t + 1], scale=gain[:, g, t : t + 1],
+                )
+            h2_grouped = stage.tile([P, PAIR_TOKENS, PACK], BF16, align_bytes=64)
+            nc.gpsimd.tensor_scalar(
+                out=h2_grouped[:], in0=h2_by_t[:].rearrange("q t r -> q r t"),
+                scalar1=1.0, scalar2=0.0, op0=ALU.mult, op1=ALU.add,
+            )
+            return h2_grouped
+
+        def quantise_h2(unit, h2_grouped):
+            j, g = divmod(unit, PASSES)
+            tokens = slice(j * PAIR_TOKENS, (j + 1) * PAIR_TOKENS)
+            nc.vector.quantize_mx(
+                out=h2_codes[:, g, tokens].bitcast(FP8X4),
+                scales=h2_scales[:, g, tokens],
+                in_=h2_grouped[:].rearrange("q r t -> q (r t)"),
+            )
+
+        def second_matmul(i):
+            tokens = slice(i * P, (i + 1) * P)
+            result = results.tile([P, OUT_DIM], F32)
+            for chunk in range(OUT_DIM // N_TILE):
+                cols = slice(chunk * N_TILE, (chunk + 1) * N_TILE)
+                acc = products.tile([P, N_TILE], F32, tag="bank")
+                for g in range(PASSES):
+                    nc.tensor.matmul_mx(
+                        out=acc[:],
+                        lhsT=h2_codes[:, g, tokens].bitcast(FP8X4),
+                        lhsT_scale=h2_scales[:, g, tokens],
+                        rhs=wo_words[:, g, cols].bitcast(FP8X4),
+                        rhs_scale=wo_planes[:, g, cols],
+                        start=(g == 0),
+                        stop=(g == PASSES - 1),
+                    )
+                nc.vector.tensor_tensor(
+                    out=result[:, cols], in0=acc[:], in1=bo_rows[:, cols], op=ALU.add
+                )
+                if chunk % 2 == 1:
+                    done = slice((chunk - 1) * N_TILE, (chunk + 1) * N_TILE)
+                    nc.sync.dma_start(out=out[tokens, done], in_=result[:, done])
+
+        h1_grouped = {0: flip_h1(0)}
+        quantise_h1(0, h1_grouped[0])
+        h2_grouped = {}
+        for tick in range(TOKEN_TILES + OUT_LAG):
+            if tick + 1 < TOKEN_TILES:
+                h1_grouped[tick + 1] = flip_h1(tick + 1)
+            if 0 <= tick - QUANT_LAG < UNITS:
+                quantise_h2(tick - QUANT_LAG, h2_grouped[tick - QUANT_LAG])
+            if 0 <= tick - GELU_LAG < UNITS:
+                h2_grouped[tick - GELU_LAG] = gelu_unit(tick - GELU_LAG)
+            if tick < TOKEN_TILES:
+                y, row_sum = first_matmul(tick)
+                normalise(tick, y, row_sum)
+            if tick + 1 < TOKEN_TILES:
+                quantise_h1(tick + 1, h1_grouped[tick + 1])
+            if 0 <= tick - OUT_LAG < TOKEN_TILES:
+                second_matmul(tick - OUT_LAG)

@@ -25,9 +25,11 @@ TOKEN_TILES = TOKENS // P
 PAIR = 2
 PAIR_TOKENS = PAIR * P
 UNITS = (TOKEN_TILES // PAIR) * PASSES
+FLIP_LEAD = 2
+NORM_LAG = 1
 GELU_LAG = 4
-QUANT_LAG = GELU_LAG + 1
-OUT_LAG = QUANT_LAG + 1
+QUANT_LAG = 6
+OUT_LAG = 8
 
 FLOPS = 2 * TOKENS * HIDDEN * HIDDEN + 2 * TOKENS * HIDDEN * OUT_DIM
 
@@ -168,10 +170,6 @@ def tile_synapsemodel_pb_kernel(
                     op1=ALU.add,
                     accum_out=row_sum[:, chunk : chunk + 1],
                 )
-            return y, row_sum
-
-        def normalise(i, y, row_sum):
-            flat = y[:].rearrange("r g t q -> r (g t q)")
             neg_mean = stats.tile([P, 1], F32)
             nc.vector.tensor_scalar(
                 out=neg_mean[:],
@@ -181,12 +179,18 @@ def tile_synapsemodel_pb_kernel(
                 op0=ALU.add,
                 op1=ALU.mult,
             )
+            return y[:].rearrange("r g t q -> r (g t q)"), neg_mean
+
+        def sum_squares(y, neg_mean):
             squares = rows.tile([P, HIDDEN], BF16)
             sum_sq = stats.tile([P, 1], F32)
             nc.scalar.activation(
-                out=squares[:], in_=flat, func=ACT.Square, bias=neg_mean[:], scale=1.0,
+                out=squares[:], in_=y, func=ACT.Square, bias=neg_mean[:], scale=1.0,
                 accum_out=sum_sq[:],
             )
+            return sum_sq
+
+        def normalise(i, y, neg_mean, sum_sq):
             var_eps = stats.tile([P, 1], F32)
             nc.gpsimd.tensor_scalar(
                 out=var_eps[:], in0=sum_sq[:], scalar1=1.0 / HIDDEN, scalar2=LN_EPS,
@@ -196,7 +200,7 @@ def tile_synapsemodel_pb_kernel(
             nc.gpsimd.tensor_tensor(out=rstd[:], in0=var_eps[:], in1=minus_half[:], op=ALU.pow)
             centred = rows.tile([P, PASSES, PACK, P], F32, bufs=6)
             nc.gpsimd.tensor_scalar(
-                out=centred[:].rearrange("r g t q -> r (g t q)"), in0=flat,
+                out=centred[:].rearrange("r g t q -> r (g t q)"), in0=y,
                 scalar1=neg_mean[:], scalar2=rstd[:], op0=ALU.add, op1=ALU.mult,
             )
             normalised[i] = centred
@@ -220,7 +224,10 @@ def tile_synapsemodel_pb_kernel(
                     out=h2_by_t[:, t, :], in_=banks[t // 2][:, t % 2, :], func=ACT.Gelu,
                     bias=shift[:, g, t : t + 1], scale=gain[:, g, t : t + 1],
                 )
-            h2_grouped = stage.tile([P, PAIR_TOKENS, PACK], BF16, align_bytes=64)
+            return h2_by_t
+
+        def regroup_h2(h2_by_t):
+            h2_grouped = stage.tile([P, PAIR_TOKENS, PACK], BF16, align_bytes=64, bufs=4)
             nc.gpsimd.tensor_scalar(
                 out=h2_grouped[:], in0=h2_by_t[:].rearrange("q t r -> q r t"),
                 scalar1=1.0, scalar2=0.0, op0=ALU.mult, op1=ALU.add,
@@ -259,20 +266,28 @@ def tile_synapsemodel_pb_kernel(
                     done = slice((chunk - 1) * N_TILE, (chunk + 1) * N_TILE)
                     nc.sync.dma_start(out=out[tokens, done], in_=result[:, done])
 
-        h1_grouped = {0: flip_h1(0)}
-        quantise_h1(0, h1_grouped[0])
+        h1_grouped = {}
+        first_product = {}
+        sums_of_squares = {}
+        h2_by_t = {}
         h2_grouped = {}
-        for tick in range(TOKEN_TILES + OUT_LAG):
-            if tick + 1 < TOKEN_TILES:
-                h1_grouped[tick + 1] = flip_h1(tick + 1)
+        for tick in range(-FLIP_LEAD, TOKEN_TILES + OUT_LAG):
+            if 0 <= tick + 1 < TOKEN_TILES:
+                quantise_h1(tick + 1, h1_grouped[tick + 1])
             if 0 <= tick - QUANT_LAG < UNITS:
                 quantise_h2(tick - QUANT_LAG, h2_grouped[tick - QUANT_LAG])
+            if 0 <= tick < TOKEN_TILES:
+                first_product[tick] = first_matmul(tick)
+            if tick + FLIP_LEAD < TOKEN_TILES:
+                h1_grouped[tick + FLIP_LEAD] = flip_h1(tick + FLIP_LEAD)
             if 0 <= tick - GELU_LAG < UNITS:
-                h2_grouped[tick - GELU_LAG] = gelu_unit(tick - GELU_LAG)
-            if tick < TOKEN_TILES:
-                y, row_sum = first_matmul(tick)
-                normalise(tick, y, row_sum)
-            if tick + 1 < TOKEN_TILES:
-                quantise_h1(tick + 1, h1_grouped[tick + 1])
+                h2_by_t[tick - GELU_LAG] = gelu_unit(tick - GELU_LAG)
+            if 0 <= tick < TOKEN_TILES:
+                sums_of_squares[tick] = sum_squares(*first_product[tick])
+            if 0 <= tick - NORM_LAG < TOKEN_TILES:
+                i = tick - NORM_LAG
+                normalise(i, *first_product[i], sums_of_squares[i])
+            if 0 <= tick - GELU_LAG < UNITS:
+                h2_grouped[tick - GELU_LAG] = regroup_h2(h2_by_t[tick - GELU_LAG])
             if 0 <= tick - OUT_LAG < TOKEN_TILES:
                 second_matmul(tick - OUT_LAG)

@@ -97,10 +97,6 @@ def tile_synapsemodel_pb_kernel(
 
         b2_rows = const.tile([P, HIDDEN], BF16)
         nc.scalar.dma_start(out=b2_rows[:], in_=b2.partition_broadcast(P))
-        b2_sorted = const.tile([P, PASSES, PACK, P], F32)
-        nc.vector.tensor_copy(
-            out=b2_sorted[:], in_=b2_rows[:].rearrange("r (g q t) -> r g t q", g=PASSES, t=PACK)
-        )
 
         def load_per_k(vector, name):
             as_bf16 = const.tile([P, PASSES, PACK], BF16, name=name + "_bf16")
@@ -162,10 +158,10 @@ def tile_synapsemodel_pb_kernel(
                         stop=(g == PASSES - 1),
                     )
                 nc.vector.scalar_tensor_tensor(
-                    out=y[:, chunk],
-                    in0=acc[:].rearrange("r (q t) -> r t q", t=PACK),
+                    out=y[:, chunk].rearrange("r t q -> r q t"),
+                    in0=acc[:].rearrange("r (q t) -> r q t", t=PACK),
                     scalar=1.0,
-                    in1=b2_sorted[:, chunk],
+                    in1=b2_rows[:, cols].rearrange("r (q t) -> r q t", t=PACK),
                     op0=ALU.mult,
                     op1=ALU.add,
                     accum_out=row_sum[:, chunk : chunk + 1],

@@ -26,8 +26,9 @@ PAIR = 2
 PAIR_TOKENS = PAIR * P
 UNITS = (TOKEN_TILES // PAIR) * PASSES
 FLIP_LEAD = 2
-NORM_LAG = 1
-GELU_LAG = 4
+STATS_LAG = 1
+NORM_LAG = 3
+GELU_LAG = 5
 QUANT_LAG = 6
 OUT_LAG = 8
 
@@ -43,7 +44,7 @@ def tile_synapsemodel_pb_kernel(
         keep = ctx.enter_context(tc.tile_pool(name="keep", bufs=1))
         stage = ctx.enter_context(tc.tile_pool(name="stage", bufs=3))
         rows = ctx.enter_context(tc.tile_pool(name="rows", bufs=4))
-        stats = ctx.enter_context(tc.tile_pool(name="stats", bufs=4))
+        stats = ctx.enter_context(tc.tile_pool(name="stats", bufs=6))
         results = ctx.enter_context(tc.tile_pool(name="results", bufs=3))
         transposed = ctx.enter_context(tc.psum_pool(name="transposed", bufs=4))
         products = ctx.enter_context(tc.psum_pool(name="products", bufs=4))
@@ -186,7 +187,7 @@ def tile_synapsemodel_pb_kernel(
             )
             return sum_sq
 
-        def normalise(i, y, neg_mean, sum_sq):
+        def inverse_std(sum_sq):
             var_eps = stats.tile([P, 1], F32)
             nc.gpsimd.tensor_scalar(
                 out=var_eps[:], in0=sum_sq[:], scalar1=1.0 / HIDDEN, scalar2=LN_EPS,
@@ -194,8 +195,11 @@ def tile_synapsemodel_pb_kernel(
             )
             rstd = stats.tile([P, 1], F32)
             nc.gpsimd.tensor_tensor(out=rstd[:], in0=var_eps[:], in1=minus_half[:], op=ALU.pow)
+            return rstd
+
+        def normalise(i, y, neg_mean, rstd):
             centred = rows.tile([P, PASSES, PACK, P], F32, bufs=6)
-            nc.gpsimd.tensor_scalar(
+            nc.vector.tensor_scalar(
                 out=centred[:].rearrange("r g t q -> r (g t q)"), in0=y,
                 scalar1=neg_mean[:], scalar2=rstd[:], op0=ALU.add, op1=ALU.mult,
             )
@@ -224,9 +228,9 @@ def tile_synapsemodel_pb_kernel(
 
         def regroup_h2(h2_by_t):
             h2_grouped = stage.tile([P, PAIR_TOKENS, PACK], BF16, align_bytes=64, bufs=4)
-            nc.gpsimd.tensor_scalar(
-                out=h2_grouped[:], in0=h2_by_t[:].rearrange("q t r -> q r t"),
-                scalar1=1.0, scalar2=0.0, op0=ALU.mult, op1=ALU.add,
+            nc.scalar.copy(
+                out=h2_grouped[:].rearrange("q (c i) t -> q c t i", i=PACK),
+                in_=h2_by_t[:].rearrange("q t (c i) -> q c t i", i=PACK),
             )
             return h2_grouped
 
@@ -264,26 +268,24 @@ def tile_synapsemodel_pb_kernel(
 
         h1_grouped = {}
         first_product = {}
-        sums_of_squares = {}
-        h2_by_t = {}
+        inverse_stds = {}
         h2_grouped = {}
         for tick in range(-FLIP_LEAD, TOKEN_TILES + OUT_LAG):
             if 0 <= tick + 1 < TOKEN_TILES:
                 quantise_h1(tick + 1, h1_grouped[tick + 1])
             if 0 <= tick - QUANT_LAG < UNITS:
                 quantise_h2(tick - QUANT_LAG, h2_grouped[tick - QUANT_LAG])
+            if 0 <= tick - NORM_LAG < TOKEN_TILES:
+                i = tick - NORM_LAG
+                normalise(i, *first_product[i], inverse_stds[i])
             if 0 <= tick < TOKEN_TILES:
                 first_product[tick] = first_matmul(tick)
             if tick + FLIP_LEAD < TOKEN_TILES:
                 h1_grouped[tick + FLIP_LEAD] = flip_h1(tick + FLIP_LEAD)
             if 0 <= tick - GELU_LAG < UNITS:
-                h2_by_t[tick - GELU_LAG] = gelu_unit(tick - GELU_LAG)
-            if 0 <= tick < TOKEN_TILES:
-                sums_of_squares[tick] = sum_squares(*first_product[tick])
-            if 0 <= tick - NORM_LAG < TOKEN_TILES:
-                i = tick - NORM_LAG
-                normalise(i, *first_product[i], sums_of_squares[i])
-            if 0 <= tick - GELU_LAG < UNITS:
-                h2_grouped[tick - GELU_LAG] = regroup_h2(h2_by_t[tick - GELU_LAG])
+                h2_grouped[tick - GELU_LAG] = regroup_h2(gelu_unit(tick - GELU_LAG))
+            if 0 <= tick - STATS_LAG < TOKEN_TILES:
+                i = tick - STATS_LAG
+                inverse_stds[i] = inverse_std(sum_squares(*first_product[i]))
             if 0 <= tick - OUT_LAG < TOKEN_TILES:
                 second_matmul(tick - OUT_LAG)

@@ -55,7 +55,6 @@ def tile_synapsemodel_pb_kernel(
         wo_words = const.tile([P, PASSES, OUT_DIM], U32, align_bytes=64)
         wo_planes = const.tile([P, PASSES, OUT_DIM], U8, align_bytes=64)
         nc.vector.memset(w2_planes[:].bitcast(I32), 0)
-        nc.vector.memset(wo_planes[:].bitcast(I32), 0)
 
         def load_words(words, dram, cols):
             source = dram.rearrange("g p n t -> p g (n t)").bitcast(I32)
@@ -78,39 +77,48 @@ def tile_synapsemodel_pb_kernel(
         def load_h1(i):
             nc.sync.dma_start(out=h1_sb[i][:], in_=h1_tiles[i])
 
-        load_h1(0)
-        load_h1(1)
-        load_words(w2_words, w2_deq_words, slice(0, N_TILE))
-        load_scale_rows(w2_planes, w2_deq_scales)
-        load_words(w2_words, w2_deq_words, slice(N_TILE, HIDDEN))
-        for i in range(2, TOKEN_TILES):
-            load_h1(i)
-        load_scale_rows(wo_planes, Wo_scales)
-        load_words(wo_words, Wo_words, slice(0, OUT_DIM // 2))
-        load_words(wo_words, Wo_words, slice(OUT_DIM // 2, OUT_DIM))
-        bo_rows = const.tile([P, OUT_DIM], BF16)
-        nc.sync.dma_start(out=bo_rows[:], in_=bo.partition_broadcast(P))
-
         identity = const.tile([P, P], F32)
         make_identity(nc, identity[:])
         minus_half = const.tile([P, 1], F32)
         nc.gpsimd.memset(minus_half[:], -0.5)
-
-        b2_rows = const.tile([P, HIDDEN], BF16)
-        nc.scalar.dma_start(out=b2_rows[:], in_=b2.partition_broadcast(P))
+        ones = const.tile([P, P], BF16)
+        nc.gpsimd.memset(ones[:], 1.0)
+        b2_row = const.tile([P, HIDDEN], BF16)
+        nc.vector.memset(b2_row[:], 0.0)
+        nc.vector.memset(wo_planes[:].bitcast(I32), 0)
 
         def load_per_k(vector, name):
             as_bf16 = const.tile([P, PASSES, PACK], BF16, name=name + "_bf16")
             with nc.allow_non_contiguous_dma(reason="8-byte runs of a 2 KiB vector, once"):
-                nc.scalar.dma_start(
+                nc.sync.dma_start(
                     out=as_bf16[:], in_=vector.rearrange("(g q t) -> q g t", g=PASSES, t=PACK)
                 )
             as_f32 = const.tile([P, PASSES, PACK], F32, name=name)
             nc.gpsimd.tensor_copy(out=as_f32[:], in_=as_bf16[:])
             return as_f32
 
+        load_h1(0)
+        nc.sync.dma_start(out=b2_row[0:1, :], in_=b2.unsqueeze(0))
+        load_scale_rows(w2_planes, w2_deq_scales)
+        load_words(w2_words, w2_deq_words, slice(0, HIDDEN))
+        for i in range(1, TOKEN_TILES):
+            load_h1(i)
         gain = load_per_k(g2, "gain")
         shift = load_per_k(b2_ln, "shift")
+        load_scale_rows(wo_planes, Wo_scales)
+        load_words(wo_words, Wo_words, slice(0, OUT_DIM // 2))
+        load_words(wo_words, Wo_words, slice(OUT_DIM // 2, OUT_DIM))
+        bo_rows = const.tile([P, OUT_DIM], BF16)
+        nc.sync.dma_start(out=bo_rows[:], in_=bo.partition_broadcast(P))
+
+        b2_rows = const.tile([P, HIDDEN], F32)
+
+        def spread_b2():
+            for chunk in range(HIDDEN // N_TILE):
+                cols = slice(chunk * N_TILE, (chunk + 1) * N_TILE)
+                spread = products.tile([P, N_TILE], F32, tag="bank")
+                nc.tensor.matmul(out=spread[:], lhsT=ones[:], rhs=b2_row[:, cols], start=True, stop=True)
+                nc.scalar.copy(out=b2_rows[:, cols], in_=spread[:])
 
         h1_codes = keep.tile([P, TOKEN_TILES, PASSES * P], U32, align_bytes=64)
         h1_scales = keep.tile([P, TOKEN_TILES, PASSES * P], U8, align_bytes=64)
@@ -282,6 +290,8 @@ def tile_synapsemodel_pb_kernel(
                 first_product[tick] = first_matmul(tick)
             if tick + FLIP_LEAD < TOKEN_TILES:
                 h1_grouped[tick + FLIP_LEAD] = flip_h1(tick + FLIP_LEAD)
+            if tick == -FLIP_LEAD:
+                spread_b2()
             if 0 <= tick - GELU_LAG < UNITS:
                 h2_grouped[tick - GELU_LAG] = regroup_h2(gelu_unit(tick - GELU_LAG))
             if 0 <= tick - STATS_LAG < TOKEN_TILES:

@@ -26,10 +26,9 @@ PAIR = 2
 PAIR_TOKENS = PAIR * P
 UNITS = (TOKEN_TILES // PAIR) * PASSES
 FLIP_LEAD = 2
-STATS_LAG = 1
-NORM_LAG = 3
-GELU_LAG = 5
-QUANT_LAG = 6
+NORM_LAG = 2
+GELU_LAG = 4
+QUANT_LAG = 5
 OUT_LAG = 8
 
 FLOPS = 2 * TOKENS * HIDDEN * HIDDEN + 2 * TOKENS * HIDDEN * OUT_DIM
@@ -81,6 +80,8 @@ def tile_synapsemodel_pb_kernel(
         make_identity(nc, identity[:])
         minus_half = const.tile([P, 1], F32)
         nc.gpsimd.memset(minus_half[:], -0.5)
+        first_gelu = const.tile([P, 1], F32)
+        nc.scalar.activation(out=first_gelu[:], in_=minus_half[:], func=ACT.Gelu)
         ones = const.tile([P, P], BF16)
         nc.gpsimd.memset(ones[:], 1.0)
         b2_row = const.tile([P, HIDDEN], BF16)
@@ -281,21 +282,20 @@ def tile_synapsemodel_pb_kernel(
         for tick in range(-FLIP_LEAD, TOKEN_TILES + OUT_LAG):
             if 0 <= tick + 1 < TOKEN_TILES:
                 quantise_h1(tick + 1, h1_grouped[tick + 1])
-            if 0 <= tick - QUANT_LAG < UNITS:
-                quantise_h2(tick - QUANT_LAG, h2_grouped[tick - QUANT_LAG])
+            if 0 <= tick < TOKEN_TILES:
+                first_product[tick] = first_matmul(tick)
+            if 0 <= tick - OUT_LAG < TOKEN_TILES:
+                second_matmul(tick - OUT_LAG)
             if 0 <= tick - NORM_LAG < TOKEN_TILES:
                 i = tick - NORM_LAG
                 normalise(i, *first_product[i], inverse_stds[i])
-            if 0 <= tick < TOKEN_TILES:
-                first_product[tick] = first_matmul(tick)
             if tick + FLIP_LEAD < TOKEN_TILES:
                 h1_grouped[tick + FLIP_LEAD] = flip_h1(tick + FLIP_LEAD)
             if tick == -FLIP_LEAD:
                 spread_b2()
             if 0 <= tick - GELU_LAG < UNITS:
                 h2_grouped[tick - GELU_LAG] = regroup_h2(gelu_unit(tick - GELU_LAG))
-            if 0 <= tick - STATS_LAG < TOKEN_TILES:
-                i = tick - STATS_LAG
-                inverse_stds[i] = inverse_std(sum_squares(*first_product[i]))
-            if 0 <= tick - OUT_LAG < TOKEN_TILES:
-                second_matmul(tick - OUT_LAG)
+            if 0 <= tick < TOKEN_TILES:
+                inverse_stds[tick] = inverse_std(sum_squares(*first_product[tick]))
+            if 0 <= tick - QUANT_LAG < UNITS:
+                quantise_h2(tick - QUANT_LAG, h2_grouped[tick - QUANT_LAG])

@@ -237,9 +237,9 @@ def tile_synapsemodel_pb_kernel(
 
         def regroup_h2(h2_by_t):
             h2_grouped = stage.tile([P, PAIR_TOKENS, PACK], BF16, align_bytes=64, bufs=4)
-            nc.scalar.copy(
-                out=h2_grouped[:].rearrange("q (c i) t -> q c t i", i=PACK),
-                in_=h2_by_t[:].rearrange("q t (c i) -> q c t i", i=PACK),
+            nc.gpsimd.tensor_scalar(
+                out=h2_grouped[:], in0=h2_by_t[:].rearrange("q t r -> q r t"),
+                scalar1=1.0, scalar2=0.0, op0=ALU.mult, op1=ALU.add,
             )
             return h2_grouped
 

@@ -112,14 +112,16 @@ def tile_synapsemodel_pb_kernel(
         bo_rows = const.tile([P, OUT_DIM], BF16)
         nc.sync.dma_start(out=bo_rows[:], in_=bo.partition_broadcast(P))
 
-        b2_rows = const.tile([P, HIDDEN], F32)
+        b2_rows = const.tile([P, PASSES, PACK, P], F32)
 
         def spread_b2():
             for chunk in range(HIDDEN // N_TILE):
                 cols = slice(chunk * N_TILE, (chunk + 1) * N_TILE)
                 spread = products.tile([P, N_TILE], F32, tag="bank")
                 nc.tensor.matmul(out=spread[:], lhsT=ones[:], rhs=b2_row[:, cols], start=True, stop=True)
-                nc.scalar.copy(out=b2_rows[:, cols], in_=spread[:])
+                nc.scalar.copy(
+                    out=b2_rows[:, chunk], in_=spread[:].rearrange("r (q t) -> r t q", t=PACK)
+                )
 
         h1_codes = keep.tile([P, TOKEN_TILES, PASSES * P], U32, align_bytes=64)
         h1_scales = keep.tile([P, TOKEN_TILES, PASSES * P], U8, align_bytes=64)
@@ -168,10 +170,10 @@ def tile_synapsemodel_pb_kernel(
                         stop=(g == PASSES - 1),
                     )
                 nc.vector.scalar_tensor_tensor(
-                    out=y[:, chunk].rearrange("r t q -> r q t"),
-                    in0=acc[:].rearrange("r (q t) -> r q t", t=PACK),
+                    out=y[:, chunk],
+                    in0=acc[:].rearrange("r (q t) -> r t q", t=PACK),
                     scalar=1.0,
-                    in1=b2_rows[:, cols].rearrange("r (q t) -> r q t", t=PACK),
+                    in1=b2_rows[:, chunk],
                     op0=ALU.mult,
                     op1=ALU.add,
                     accum_out=row_sum[:, chunk : chunk + 1],

@@ -25,7 +25,8 @@ TOKEN_TILES = TOKENS // P
 PAIR = 2
 PAIR_TOKENS = PAIR * P
 UNITS = (TOKEN_TILES // PAIR) * PASSES
-FLIP_LEAD = 2
+FLIP_LEAD = 3
+QUANT_LEAD = 2
 NORM_LAG = 2
 GELU_LAG = 4
 QUANT_LAG = 5
@@ -41,10 +42,10 @@ def tile_synapsemodel_pb_kernel(
     with ExitStack() as ctx:
         const = ctx.enter_context(tc.tile_pool(name="const", bufs=1))
         keep = ctx.enter_context(tc.tile_pool(name="keep", bufs=1))
-        stage = ctx.enter_context(tc.tile_pool(name="stage", bufs=3))
+        stage = ctx.enter_context(tc.tile_pool(name="stage", bufs=4))
         rows = ctx.enter_context(tc.tile_pool(name="rows", bufs=4))
         stats = ctx.enter_context(tc.tile_pool(name="stats", bufs=6))
-        results = ctx.enter_context(tc.tile_pool(name="results", bufs=3))
+        results = ctx.enter_context(tc.tile_pool(name="results", bufs=6))
         transposed = ctx.enter_context(tc.psum_pool(name="transposed", bufs=4))
         products = ctx.enter_context(tc.psum_pool(name="products", bufs=4))
         ctx.enter_context(tc.manual_schedule())
@@ -53,7 +54,10 @@ def tile_synapsemodel_pb_kernel(
         w2_planes = const.tile([P, PASSES, HIDDEN], U8, align_bytes=64)
         wo_words = const.tile([P, PASSES, OUT_DIM], U32, align_bytes=64)
         wo_planes = const.tile([P, PASSES, OUT_DIM], U8, align_bytes=64)
+        b2_row = const.tile([P, HIDDEN], BF16)
+        nc.vector.memset(b2_row[:].bitcast(I32), 0)
         nc.vector.memset(w2_planes[:].bitcast(I32), 0)
+        nc.vector.memset(wo_planes[:].bitcast(I32), 0)
 
         def load_words(words, dram, cols):
             source = dram.rearrange("g p n t -> p g (n t)").bitcast(I32)
@@ -67,26 +71,25 @@ def tile_synapsemodel_pb_kernel(
                     in_=source[:, 4 * quadrant : 4 * quadrant + 4, :].rearrange("g r n -> r g n"),
                 )
 
-        h1_tiles = h1.rearrange("(i r) k -> i r k", r=P)
-        h1_sb = []
-        for i in range(TOKEN_TILES):
-            h1_tile = const.tile([P, HIDDEN], BF16, name="h1_tile_%d" % i)
-            h1_sb.append(h1_tile)
+        h1_tiles = h1.rearrange("(r i) k -> r i k", i=TOKEN_TILES)
+        out_tiles = out.rearrange("(r i) n -> i r n", i=TOKEN_TILES)
+        h1_sb = {}
 
-        def load_h1(i):
-            nc.sync.dma_start(out=h1_sb[i][:], in_=h1_tiles[i])
+        def load_h1(first, count):
+            h1_run = const.tile([P, count, HIDDEN], BF16, name="h1_run_%d" % first)
+            nc.sync.dma_start(out=h1_run[:], in_=h1_tiles[:, first : first + count, :])
+            for i in range(count):
+                h1_sb[first + i] = h1_run[:, i, :]
 
         identity = const.tile([P, P], F32)
         make_identity(nc, identity[:])
         minus_half = const.tile([P, 1], F32)
         nc.gpsimd.memset(minus_half[:], -0.5)
+        nc.scalar.dma_start(out=b2_row[0:1, :], in_=b2.unsqueeze(0))
         first_gelu = const.tile([P, 1], F32)
         nc.scalar.activation(out=first_gelu[:], in_=minus_half[:], func=ACT.Gelu)
         ones = const.tile([P, P], BF16)
         nc.gpsimd.memset(ones[:], 1.0)
-        b2_row = const.tile([P, HIDDEN], BF16)
-        nc.vector.memset(b2_row[:], 0.0)
-        nc.vector.memset(wo_planes[:].bitcast(I32), 0)
 
         def load_per_k(vector, name):
             as_bf16 = const.tile([P, PASSES, PACK], BF16, name=name + "_bf16")
@@ -98,12 +101,13 @@ def tile_synapsemodel_pb_kernel(
             nc.gpsimd.tensor_copy(out=as_f32[:], in_=as_bf16[:])
             return as_f32
 
-        load_h1(0)
-        nc.sync.dma_start(out=b2_row[0:1, :], in_=b2.unsqueeze(0))
+        load_h1(0, 1)
+        load_h1(1, 2)
         load_scale_rows(w2_planes, w2_deq_scales)
-        load_words(w2_words, w2_deq_words, slice(0, HIDDEN))
-        for i in range(1, TOKEN_TILES):
-            load_h1(i)
+        load_words(w2_words, w2_deq_words, slice(0, N_TILE))
+        load_words(w2_words, w2_deq_words, slice(N_TILE, HIDDEN))
+        load_h1(3, 2)
+        load_h1(5, 3)
         gain = load_per_k(g2, "gain")
         shift = load_per_k(b2_ln, "shift")
         load_scale_rows(wo_planes, Wo_scales)
@@ -130,7 +134,7 @@ def tile_synapsemodel_pb_kernel(
         normalised = {}
 
         def flip_h1(i):
-            pairs_of_k = h1_sb[i][:].bitcast(F32)
+            pairs_of_k = h1_sb[i].bitcast(F32)
             flipped = transposed.tile([P, PASSES, 2, P], F32, tag="bank")
             for g in range(PASSES):
                 for u in range(2):
@@ -178,6 +182,9 @@ def tile_synapsemodel_pb_kernel(
                     op1=ALU.add,
                     accum_out=row_sum[:, chunk : chunk + 1],
                 )
+            return y[:].rearrange("r g t q -> r (g t q)"), row_sum
+
+        def negative_mean(row_sum):
             neg_mean = stats.tile([P, 1], F32)
             nc.vector.tensor_scalar(
                 out=neg_mean[:],
@@ -187,7 +194,7 @@ def tile_synapsemodel_pb_kernel(
                 op0=ALU.add,
                 op1=ALU.mult,
             )
-            return y[:].rearrange("r g t q -> r (g t q)"), neg_mean
+            return neg_mean
 
         def sum_squares(y, neg_mean):
             squares = rows.tile([P, HIDDEN], BF16)
@@ -275,29 +282,39 @@ def tile_synapsemodel_pb_kernel(
                 )
                 if chunk % 2 == 1:
                     done = slice((chunk - 1) * N_TILE, (chunk + 1) * N_TILE)
-                    nc.sync.dma_start(out=out[tokens, done], in_=result[:, done])
+                    nc.sync.dma_start(out=out_tiles[i][:, done], in_=result[:, done])
 
         h1_grouped = {}
         first_product = {}
         inverse_stds = {}
         h2_grouped = {}
-        for tick in range(-FLIP_LEAD, TOKEN_TILES + OUT_LAG):
-            if 0 <= tick + 1 < TOKEN_TILES:
-                quantise_h1(tick + 1, h1_grouped[tick + 1])
-            if 0 <= tick < TOKEN_TILES:
-                first_product[tick] = first_matmul(tick)
+
+        def flip(i):
+            if i < TOKEN_TILES:
+                h1_grouped[i] = flip_h1(i)
+
+        flip(0)
+        spread_b2()
+        for i in range(1, FLIP_LEAD):
+            flip(i)
+        for i in range(QUANT_LEAD):
+            quantise_h1(i, h1_grouped[i])
+        for tick in range(TOKEN_TILES + OUT_LAG):
+            if tick < TOKEN_TILES:
+                y, row_sum = first_matmul(tick)
+            if tick + QUANT_LEAD < TOKEN_TILES:
+                quantise_h1(tick + QUANT_LEAD, h1_grouped[tick + QUANT_LEAD])
+            if tick < TOKEN_TILES:
+                first_product[tick] = (y, negative_mean(row_sum))
             if 0 <= tick - OUT_LAG < TOKEN_TILES:
                 second_matmul(tick - OUT_LAG)
             if 0 <= tick - NORM_LAG < TOKEN_TILES:
                 i = tick - NORM_LAG
                 normalise(i, *first_product[i], inverse_stds[i])
-            if tick + FLIP_LEAD < TOKEN_TILES:
-                h1_grouped[tick + FLIP_LEAD] = flip_h1(tick + FLIP_LEAD)
-            if tick == -FLIP_LEAD:
-                spread_b2()
+            flip(tick + FLIP_LEAD)
             if 0 <= tick - GELU_LAG < UNITS:
                 h2_grouped[tick - GELU_LAG] = regroup_h2(gelu_unit(tick - GELU_LAG))
-            if 0 <= tick < TOKEN_TILES:
+            if tick < TOKEN_TILES:
                 inverse_stds[tick] = inverse_std(sum_squares(*first_product[tick]))
             if 0 <= tick - QUANT_LAG < UNITS:
                 quantise_h2(tick - QUANT_LAG, h2_grouped[tick - QUANT_LAG])

@@ -25,6 +25,7 @@ TOKEN_TILES = TOKENS // P
 PAIR = 2
 PAIR_TOKENS = PAIR * P
 UNITS = (TOKEN_TILES // PAIR) * PASSES
+SCALAR_REGROUPS_FROM = UNITS // 2
 FLIP_LEAD = 3
 QUANT_LEAD = 2
 NORM_LAG = 2
@@ -244,12 +245,16 @@ def tile_synapsemodel_pb_kernel(
                 )
             return h2_by_t
 
-        def regroup_h2(h2_by_t):
+        def regroup_h2(unit, h2_by_t):
             h2_grouped = stage.tile([P, PAIR_TOKENS, PACK], BF16, align_bytes=64, bufs=4)
-            nc.gpsimd.tensor_scalar(
-                out=h2_grouped[:], in0=h2_by_t[:].rearrange("q t r -> q r t"),
-                scalar1=1.0, scalar2=0.0, op0=ALU.mult, op1=ALU.add,
-            )
+            by_token = h2_by_t[:].rearrange("q t r -> q r t")
+            if unit < SCALAR_REGROUPS_FROM:
+                nc.gpsimd.tensor_scalar(
+                    out=h2_grouped[:], in0=by_token, scalar1=1.0, scalar2=0.0,
+                    op0=ALU.mult, op1=ALU.add,
+                )
+            else:
+                nc.scalar.copy(out=h2_grouped[:], in_=by_token)
             return h2_grouped
 
         def quantise_h2(unit, h2_grouped):
@@ -313,7 +318,8 @@ def tile_synapsemodel_pb_kernel(
                 normalise(i, *first_product[i], inverse_stds[i])
             flip(tick + FLIP_LEAD)
             if 0 <= tick - GELU_LAG < UNITS:
-                h2_grouped[tick - GELU_LAG] = regroup_h2(gelu_unit(tick - GELU_LAG))
+                unit = tick - GELU_LAG
+                h2_grouped[unit] = regroup_h2(unit, gelu_unit(unit))
             if tick < TOKEN_TILES:
                 inverse_stds[tick] = inverse_std(sum_squares(*first_product[tick]))
             if 0 <= tick - QUANT_LAG < UNITS:

from contextlib import ExitStack

import concourse.mybir as mybir
from concourse.masks import make_identity

F32 = mybir.dt.float32
BF16 = mybir.dt.bfloat16
I32 = mybir.dt.int32
U32 = mybir.dt.uint32
U8 = mybir.dt.uint8
FP8X4 = mybir.dt.float8_e4m3fn_x4
ACT = mybir.ActivationFunctionType
ALU = mybir.AluOpType

P = 128
PACK = 4
K_PASS = P * PACK
N_TILE = 512
TOKENS = 1024
HIDDEN = 1024
OUT_DIM = 2048
LN_EPS = 1e-5
PASSES = HIDDEN // K_PASS
TOKEN_TILES = TOKENS // P
PAIR = 2
PAIR_TOKENS = PAIR * P
UNITS = (TOKEN_TILES // PAIR) * PASSES
SCALAR_REGROUPS_FROM = UNITS // 2
FLIP_LEAD = 3
QUANT_LEAD = 2
NORM_LAG = 2
GELU_LAG = 4
QUANT_LAG = 5
OUT_LAG = 8

FLOPS = 2 * TOKENS * HIDDEN * HIDDEN + 2 * TOKENS * HIDDEN * OUT_DIM


def tile_synapsemodel_pb_kernel(
    tc, h1, w2_deq_words, w2_deq_scales, b2, g2, b2_ln, Wo_words, Wo_scales, bo, out
):
    nc = tc.nc
    with ExitStack() as ctx:
        const = ctx.enter_context(tc.tile_pool(name="const", bufs=1))
        keep = ctx.enter_context(tc.tile_pool(name="keep", bufs=1))
        stage = ctx.enter_context(tc.tile_pool(name="stage", bufs=4))
        rows = ctx.enter_context(tc.tile_pool(name="rows", bufs=4))
        stats = ctx.enter_context(tc.tile_pool(name="stats", bufs=6))
        results = ctx.enter_context(tc.tile_pool(name="results", bufs=6))
        transposed = ctx.enter_context(tc.psum_pool(name="transposed", bufs=4))
        products = ctx.enter_context(tc.psum_pool(name="products", bufs=4))
        ctx.enter_context(tc.manual_schedule())

        w2_words = const.tile([P, PASSES, HIDDEN], U32, align_bytes=64)
        w2_planes = const.tile([P, PASSES, HIDDEN], U8, align_bytes=64)
        wo_words = const.tile([P, PASSES, OUT_DIM], U32, align_bytes=64)
        wo_planes = const.tile([P, PASSES, OUT_DIM], U8, align_bytes=64)
        b2_row = const.tile([P, HIDDEN], BF16)
        nc.vector.memset(b2_row[:].bitcast(I32), 0)
        nc.vector.memset(w2_planes[:].bitcast(I32), 0)
        nc.vector.memset(wo_planes[:].bitcast(I32), 0)

        def load_words(words, dram, cols):
            source = dram.rearrange("g p n t -> p g (n t)").bitcast(I32)
            nc.sync.dma_start(out=words[:, :, cols].bitcast(I32), in_=source[:, :, cols])

        def load_scale_rows(planes, dram):
            source = dram.bitcast(I32)
            for quadrant in range(4):
                nc.sync.dma_start(
                    out=planes[32 * quadrant : 32 * quadrant + 4].bitcast(I32),
                    in_=source[:, 4 * quadrant : 4 * quadrant + 4, :].rearrange("g r n -> r g n"),
                )

        h1_tiles = h1.rearrange("(r i) k -> r i k", i=TOKEN_TILES)
        out_tiles = out.rearrange("(r i) n -> i r n", i=TOKEN_TILES)
        h1_sb = {}

        def load_h1(first, count):
            h1_run = const.tile([P, count, HIDDEN], BF16, name="h1_run_%d" % first)
            nc.sync.dma_start(out=h1_run[:], in_=h1_tiles[:, first : first + count, :])
            for i in range(count):
                h1_sb[first + i] = h1_run[:, i, :]

        identity = const.tile([P, P], F32)
        make_identity(nc, identity[:])
        minus_half = const.tile([P, 1], F32)
        nc.gpsimd.memset(minus_half[:], -0.5)
        nc.scalar.dma_start(out=b2_row[0:1, :], in_=b2.unsqueeze(0))
        first_gelu = const.tile([P, 1], F32)
        nc.scalar.activation(out=first_gelu[:], in_=minus_half[:], func=ACT.Gelu)
        ones = const.tile([P, P], BF16)
        nc.gpsimd.memset(ones[:], 1.0)

        def load_per_k(vector, name):
            as_bf16 = const.tile([P, PASSES, PACK], BF16, name=name + "_bf16")
            with nc.allow_non_contiguous_dma(reason="8-byte runs of a 2 KiB vector, once"):
                nc.sync.dma_start(
                    out=as_bf16[:], in_=vector.rearrange("(g q t) -> q g t", g=PASSES, t=PACK)
                )
            as_f32 = const.tile([P, PASSES, PACK], F32, name=name)
            nc.gpsimd.tensor_copy(out=as_f32[:], in_=as_bf16[:])
            return as_f32

        load_h1(0, 1)
        load_h1(1, 2)
        load_scale_rows(w2_planes, w2_deq_scales)
        load_words(w2_words, w2_deq_words, slice(0, N_TILE))
        load_words(w2_words, w2_deq_words, slice(N_TILE, HIDDEN))
        load_h1(3, 2)
        load_h1(5, 3)
        gain = load_per_k(g2, "gain")
        shift = load_per_k(b2_ln, "shift")
        load_scale_rows(wo_planes, Wo_scales)
        load_words(wo_words, Wo_words, slice(0, OUT_DIM // 2))
        load_words(wo_words, Wo_words, slice(OUT_DIM // 2, OUT_DIM))
        bo_rows = const.tile([P, OUT_DIM], BF16)
        nc.sync.dma_start(out=bo_rows[:], in_=bo.partition_broadcast(P))

        b2_rows = const.tile([P, PASSES, PACK, P], F32)

        def spread_b2():
            for chunk in range(HIDDEN // N_TILE):
                cols = slice(chunk * N_TILE, (chunk + 1) * N_TILE)
                spread = products.tile([P, N_TILE], F32, tag="bank")
                nc.tensor.matmul(out=spread[:], lhsT=ones[:], rhs=b2_row[:, cols], start=True, stop=True)
                nc.scalar.copy(
                    out=b2_rows[:, chunk], in_=spread[:].rearrange("r (q t) -> r t q", t=PACK)
                )

        h1_codes = keep.tile([P, TOKEN_TILES, PASSES * P], U32, align_bytes=64)
        h1_scales = keep.tile([P, TOKEN_TILES, PASSES * P], U8, align_bytes=64)
        h2_codes = keep.tile([P, PASSES, TOKENS], U32, align_bytes=64)
        h2_scales = keep.tile([P, PASSES, TOKENS], U8, align_bytes=64)
        normalised = {}

        def flip_h1(i):
            pairs_of_k = h1_sb[i].bitcast(F32)
            flipped = transposed.tile([P, PASSES, 2, P], F32, tag="bank")
            for g in range(PASSES):
                for u in range(2):
                    nc.tensor.transpose(
                        flipped[:, g, u, :],
                        pairs_of_k[:, 256 * g + u : 256 * (g + 1) : 2],
                        identity[:],
                    )
            grouped = stage.tile([P, PASSES, P, PACK], BF16, align_bytes=64)
            nc.scalar.copy(
                out=grouped[:].bitcast(F32), in_=flipped[:].rearrange("q g u r -> q g r u")
            )
            return grouped

        def quantise_h1(i, grouped):
            nc.vector.quantize_mx(
                out=h1_codes[:, i, :].bitcast(FP8X4),
                scales=h1_scales[:, i, :],
                in_=grouped[:].rearrange("q g r t -> q (g r t)"),
            )

        def first_matmul(i):
            y = rows.tile([P, PASSES, PACK, P], F32)
            row_sum = stats.tile([P, PASSES], F32)
            for chunk in range(HIDDEN // N_TILE):
                cols = slice(chunk * N_TILE, (chunk + 1) * N_TILE)
                acc = products.tile([P, N_TILE], F32, tag="bank")
                for g in range(PASSES):
                    of_pass = slice(g * P, (g + 1) * P)
                    nc.tensor.matmul_mx(
                        out=acc[:],
                        lhsT=h1_codes[:, i, of_pass].bitcast(FP8X4),
                        lhsT_scale=h1_scales[:, i, of_pass],
                        rhs=w2_words[:, g, cols].bitcast(FP8X4),
                        rhs_scale=w2_planes[:, g, cols],
                        start=(g == 0),
                        stop=(g == PASSES - 1),
                    )
                nc.vector.scalar_tensor_tensor(
                    out=y[:, chunk],
                    in0=acc[:].rearrange("r (q t) -> r t q", t=PACK),
                    scalar=1.0,
                    in1=b2_rows[:, chunk],
                    op0=ALU.mult,
                    op1=ALU.add,
                    accum_out=row_sum[:, chunk : chunk + 1],
                )
            return y[:].rearrange("r g t q -> r (g t q)"), row_sum

        def negative_mean(row_sum):
            neg_mean = stats.tile([P, 1], F32)
            nc.vector.tensor_scalar(
                out=neg_mean[:],
                in0=row_sum[:, 0:1],
                scalar1=row_sum[:, 1:2],
                scalar2=-1.0 / HIDDEN,
                op0=ALU.add,
                op1=ALU.mult,
            )
            return neg_mean

        def sum_squares(y, neg_mean):
            squares = rows.tile([P, HIDDEN], BF16)
            sum_sq = stats.tile([P, 1], F32)
            nc.scalar.activation(
                out=squares[:], in_=y, func=ACT.Square, bias=neg_mean[:], scale=1.0,
                accum_out=sum_sq[:],
            )
            return sum_sq

        def inverse_std(sum_sq):
            var_eps = stats.tile([P, 1], F32)
            nc.gpsimd.tensor_scalar(
                out=var_eps[:], in0=sum_sq[:], scalar1=1.0 / HIDDEN, scalar2=LN_EPS,
                op0=ALU.mult, op1=ALU.add,
            )
            rstd = stats.tile([P, 1], F32)
            nc.gpsimd.tensor_tensor(out=rstd[:], in0=var_eps[:], in1=minus_half[:], op=ALU.pow)
            return rstd

        def normalise(i, y, neg_mean, rstd):
            centred = rows.tile([P, PASSES, PACK, P], F32, bufs=6)
            nc.vector.tensor_scalar(
                out=centred[:].rearrange("r g t q -> r (g t q)"), in0=y,
                scalar1=neg_mean[:], scalar2=rstd[:], op0=ALU.add, op1=ALU.mult,
            )
            normalised[i] = centred

        def gelu_unit(unit):
            j, g = divmod(unit, PASSES)
            h2_by_t = stage.tile([P, PACK, PAIR_TOKENS], BF16)
            banks = []
            for half in range(2):
                flipped = transposed.tile([P, 2, PAIR_TOKENS], F32, tag="bank")
                banks.append(flipped)
                for u in range(2):
                    for s in range(PAIR):
                        nc.tensor.transpose(
                            flipped[:, u, s * P : (s + 1) * P],
                            normalised[PAIR * j + s][:, g, 2 * half + u, :],
                            identity[:],
                        )
            for t in range(PACK):
                nc.scalar.activation(
                    out=h2_by_t[:, t, :], in_=banks[t // 2][:, t % 2, :], func=ACT.Gelu,
                    bias=shift[:, g, t : t + 1], scale=gain[:, g, t : t + 1],
                )
            return h2_by_t

        def regroup_h2(unit, h2_by_t):
            h2_grouped = stage.tile([P, PAIR_TOKENS, PACK], BF16, align_bytes=64, bufs=4)
            by_token = h2_by_t[:].rearrange("q t r -> q r t")
            if unit < SCALAR_REGROUPS_FROM:
                nc.gpsimd.tensor_scalar(
                    out=h2_grouped[:], in0=by_token, scalar1=1.0, scalar2=0.0,
                    op0=ALU.mult, op1=ALU.add,
                )
            else:
                nc.scalar.copy(out=h2_grouped[:], in_=by_token)
            return h2_grouped

        def quantise_h2(unit, h2_grouped):
            j, g = divmod(unit, PASSES)
            tokens = slice(j * PAIR_TOKENS, (j + 1) * PAIR_TOKENS)
            nc.vector.quantize_mx(
                out=h2_codes[:, g, tokens].bitcast(FP8X4),
                scales=h2_scales[:, g, tokens],
                in_=h2_grouped[:].rearrange("q r t -> q (r t)"),
            )

        def second_matmul(i):
            tokens = slice(i * P, (i + 1) * P)
            result = results.tile([P, OUT_DIM], F32)
            for chunk in range(OUT_DIM // N_TILE):
                cols = slice(chunk * N_TILE, (chunk + 1) * N_TILE)
                acc = products.tile([P, N_TILE], F32, tag="bank")
                for g in range(PASSES):
                    nc.tensor.matmul_mx(
                        out=acc[:],
                        lhsT=h2_codes[:, g, tokens].bitcast(FP8X4),
                        lhsT_scale=h2_scales[:, g, tokens],
                        rhs=wo_words[:, g, cols].bitcast(FP8X4),
                        rhs_scale=wo_planes[:, g, cols],
                        start=(g == 0),
                        stop=(g == PASSES - 1),
                    )
                nc.vector.tensor_tensor(
                    out=result[:, cols], in0=acc[:], in1=bo_rows[:, cols], op=ALU.add
                )
                if chunk % 2 == 1:
                    done = slice((chunk - 1) * N_TILE, (chunk + 1) * N_TILE)
                    nc.sync.dma_start(out=out_tiles[i][:, done], in_=result[:, done])

        h1_grouped = {}
        first_product = {}
        inverse_stds = {}
        h2_grouped = {}

        def flip(i):
            if i < TOKEN_TILES:
                h1_grouped[i] = flip_h1(i)

        flip(0)
        spread_b2()
        for i in range(1, FLIP_LEAD):
            flip(i)
        for i in range(QUANT_LEAD):
            quantise_h1(i, h1_grouped[i])
        for tick in range(TOKEN_TILES + OUT_LAG):
            if tick < TOKEN_TILES:
                y, row_sum = first_matmul(tick)
            if tick + QUANT_LEAD < TOKEN_TILES:
                quantise_h1(tick + QUANT_LEAD, h1_grouped[tick + QUANT_LEAD])
            if tick < TOKEN_TILES:
                first_product[tick] = (y, negative_mean(row_sum))
            if 0 <= tick - OUT_LAG < TOKEN_TILES:
                second_matmul(tick - OUT_LAG)
            if 0 <= tick - NORM_LAG < TOKEN_TILES:
                i = tick - NORM_LAG
                normalise(i, *first_product[i], inverse_stds[i])
            flip(tick + FLIP_LEAD)
            if 0 <= tick - GELU_LAG < UNITS:
                unit = tick - GELU_LAG
                h2_grouped[unit] = regroup_h2(unit, gelu_unit(unit))
            if tick < TOKEN_TILES:
                inverse_stds[tick] = inverse_std(sum_squares(*first_product[tick]))
            if 0 <= tick - QUANT_LAG < UNITS:
                quantise_h2(tick - QUANT_LAG, h2_grouped[tick - QUANT_LAG])
